import numpy as np
import ml_dtypes


def mxq(x, axis, fmt="e4m3"):
    dtype, down = {"e4m3": (ml_dtypes.float8_e4m3fn, 7), "e5m2": (ml_dtypes.float8_e5m2, 14)}[fmt]
    v = np.moveaxis(np.asarray(x, np.float32).astype(ml_dtypes.bfloat16).astype(np.float64), axis, -1)
    blocks = v.reshape(v.shape[:-1] + (-1, 32))
    amax = np.abs(blocks).max(-1, keepdims=True)
    byte = np.maximum(np.where(amax > 0, np.frexp(amax)[1] - 1 + 127, 0) - down, 1)
    scale = np.exp2(byte - 127.0)
    codes = (blocks / scale).astype(np.float32).astype(dtype).astype(np.float64)
    return np.moveaxis((codes * scale).reshape(v.shape), -1, axis)


WIDE = False


def mx_kscale(k):
    if not WIDE:
        return np.ones(k)
    levels = np.array([10, -10, 5, -5, 0])
    a = np.random.permutation(np.resize(levels, k // 512 * 4)).reshape(k // 512, 4)
    idx = np.arange(k)
    return np.exp2(a[idx // 512, idx % 128 // 32])


BF16 = ml_dtypes.bfloat16


def bf(x):
    return np.asarray(x, np.float32).astype(BF16)


def f64(x):
    return np.asarray(x).astype(np.float64)


B, S, K, N = 4, 32, 1024, 1024
THRESHOLD = 0.3


def ternary_quantize(w, threshold=THRESHOLD):
    return np.sign(w) * (np.abs(w) > threshold)


def ternary_ste(w, threshold=THRESHOLD):
    return w + (ternary_quantize(w, threshold) - w)


def setup_inputs():
    s = mx_kscale(K)
    r = s / s.min()
    return {"x": bf(np.random.standard_normal((B, S, K)) * 8.0 / np.sqrt(K) * r),
            "kernel": bf(0.2 * np.random.standard_normal((K, N)) / r[:, None])}


def reference(x, kernel):
    w_ternary = ternary_ste(f64(kernel), THRESHOLD)
    return mxq(f64(x), 2, "e4m3") @ mxq(w_ternary, 0, "e4m3")

@@ -1,0 +1,137 @@
+from contextlib import ExitStack
+
+from concourse import mybir
+from concourse.masks import make_identity
+
+F32 = mybir.dt.float32
+BF16 = mybir.dt.bfloat16
+U32 = mybir.dt.uint32
+U8 = mybir.dt.uint8
+FP8X4 = mybir.dt.float8_e4m3fn_x4
+ALU = mybir.AluOpType
+ACT = mybir.ActivationFunctionType
+
+P = 128
+PACK = 4
+K_PASS = P * PACK
+TOKENS = 128
+K = 1024
+N = 1024
+PASSES = K // K_PASS
+THRESHOLD = 0.3
+
+COLS = 256
+GROUPS = N // COLS
+CHUNKS = GROUPS * PASSES
+SIGN_AHEAD = 2
+
+FLOPS = 2 * TOKENS * K * N
+
+
+def tile_ternarylinear_s_kernel(tc, x, kernel, out):
+    nc = tc.nc
+    x_rows = x.flatten_outer_dims()
+    out_rows = out.flatten_outer_dims()
+    kernel_passes = kernel.rearrange("(c p j) n -> c p j n", p=P, j=PACK)
+
+    with ExitStack() as ctx:
+        keep = ctx.enter_context(tc.tile_pool(name="keep", bufs=1))
+        raw_pool = ctx.enter_context(tc.tile_pool(name="raw", bufs=CHUNKS))
+        sign_pool = ctx.enter_context(tc.tile_pool(name="sign", bufs=SIGN_AHEAD + 2))
+        grouped_pool = ctx.enter_context(tc.tile_pool(name="grouped", bufs=3))
+        result_pool = ctx.enter_context(tc.tile_pool(name="result", bufs=GROUPS))
+        xt_pool = ctx.enter_context(tc.psum_pool(name="xt", bufs=1))
+        acc_pool = ctx.enter_context(tc.psum_pool(name="acc", bufs=GROUPS))
+
+        x_sb = keep.tile([TOKENS, K], BF16)
+        nc.sync.dma_start(out=x_sb[:], in_=x_rows)
+        raw_tiles = []
+        for g in range(GROUPS):
+            for c in range(PASSES):
+                raw = raw_pool.tile([P, PACK, COLS], BF16, name="raw")
+                nc.sync.dma_start(
+                    out=raw[:], in_=kernel_passes[c, :, :, g * COLS : (g + 1) * COLS]
+                )
+                raw_tiles.append(raw)
+
+        identity = keep.tile([P, P], F32)
+        make_identity(nc, identity[:])
+        x_words = x_sb[:].bitcast(F32).rearrange("m (c p u) -> m c u p", c=PASSES, u=2)
+        xt = xt_pool.tile([P, PASSES, 2, TOKENS], F32)
+        for c in range(PASSES):
+            for u in range(2):
+                nc.tensor.transpose(xt[:, c, u, :], x_words[:, c, u, :], identity[:])
+        x_grouped = keep.tile([P, PASSES * TOKENS * PACK], BF16, align_bytes=64)
+        nc.vector.tensor_copy(
+            out=x_grouped[:].bitcast(F32).rearrange("p (c m u) -> p c m u", c=PASSES, u=2),
+            in_=xt[:].rearrange("p c u m -> p c m u"),
+        )
+        x_codes = keep.tile([P, PASSES, TOKENS], U32, align_bytes=64)
+        x_scales = keep.tile([P, PASSES, TOKENS], U8, align_bytes=64)
+        nc.vector.quantize_mx(
+            out=x_codes[:].rearrange("p c m -> p (c m)").bitcast(FP8X4),
+            scales=x_scales[:].rearrange("p c m -> p (c m)"),
+            in_=x_grouped[:],
+        )
+
+        w_codes = keep.tile([P, CHUNKS, COLS], U32, align_bytes=64)
+        w_scales = keep.tile([P, CHUNKS, COLS], U8, align_bytes=64)
+        sign_tiles = {}
+        grouped_tiles = {}
+
+        def sign_step(i):
+            above_low = sign_pool.tile([P, PACK, COLS], BF16, name="above_low")
+            nc.scalar.activation(
+                out=above_low[:], in_=raw_tiles[i][:], func=ACT.Sign, bias=THRESHOLD
+            )
+            sign_tiles[i] = above_low
+
+        def ternary_step(i):
+            grouped = grouped_pool.tile([P, COLS, PACK], BF16, name="grouped", align_bytes=64)
+            nc.vector.scalar_tensor_tensor(
+                out=grouped[:],
+                in0=raw_tiles[i][:].rearrange("p j n -> p n j"),
+                scalar=THRESHOLD,
+                in1=sign_tiles[i][:].rearrange("p j n -> p n j"),
+                op0=ALU.is_gt,
+                op1=ALU.min,
+            )
+            grouped_tiles[i] = grouped
+
+        def quantise_step(i):
+            nc.vector.quantize_mx(
+                out=w_codes[:, i, :].bitcast(FP8X4),
+                scales=w_scales[:, i, :],
+                in_=grouped_tiles[i][:].rearrange("p n j -> p (n j)"),
+            )
+
+        def multiply_group(g):
+            acc = acc_pool.tile([TOKENS, COLS], F32, name="acc")
+            for c in range(PASSES):
+                nc.tensor.matmul_mx(
+                    out=acc[:],
+                    lhsT=x_codes[:, c, :].bitcast(FP8X4),
+                    lhsT_scale=x_scales[:, c, :],
+                    rhs=w_codes[:, g * PASSES + c, :].bitcast(FP8X4),
+                    rhs_scale=w_scales[:, g * PASSES + c, :],
+                    start=(c == 0),
+                    stop=(c == PASSES - 1),
+                )
+            result = result_pool.tile([TOKENS, COLS], F32, name="result")
+            nc.scalar.copy(out=result[:], in_=acc[:])
+            nc.sync.dma_start(out=out_rows[:, g * COLS : (g + 1) * COLS], in_=result[:])
+
+        def finish_chunk(i):
+            quantise_step(i)
+            if i % PASSES == PASSES - 1:
+                multiply_group(i // PASSES)
+
+        for i in range(SIGN_AHEAD):
+            sign_step(i)
+        for i in range(CHUNKS):
+            if i + SIGN_AHEAD < CHUNKS:
+                sign_step(i + SIGN_AHEAD)
+            ternary_step(i)
+            if i > 0:
+                finish_chunk(i - 1)
+        finish_chunk(CHUNKS - 1)

@@ -23,7 +23,8 @@ THRESHOLD = 0.3
 COLS = 256
 GROUPS = N // COLS
 CHUNKS = GROUPS * PASSES
-SIGN_AHEAD = 2
+INV_TWICE_THRESHOLD = 1.0 / (2.0 * THRESHOLD)
+ROUND_MAGIC = 1.5 * 2.0**23
 
 FLOPS = 2 * TOKENS * K * N
 
@@ -37,14 +38,13 @@ def tile_ternarylinear_s_kernel(tc, x, kernel, out):
     with ExitStack() as ctx:
         keep = ctx.enter_context(tc.tile_pool(name="keep", bufs=1))
         raw_pool = ctx.enter_context(tc.tile_pool(name="raw", bufs=CHUNKS))
-        sign_pool = ctx.enter_context(tc.tile_pool(name="sign", bufs=SIGN_AHEAD + 2))
+        rounded_pool = ctx.enter_context(tc.tile_pool(name="rounded", bufs=3))
         grouped_pool = ctx.enter_context(tc.tile_pool(name="grouped", bufs=3))
         result_pool = ctx.enter_context(tc.tile_pool(name="result", bufs=GROUPS))
         xt_pool = ctx.enter_context(tc.psum_pool(name="xt", bufs=1))
         acc_pool = ctx.enter_context(tc.psum_pool(name="acc", bufs=GROUPS))
 
         x_sb = keep.tile([TOKENS, K], BF16)
-        nc.sync.dma_start(out=x_sb[:], in_=x_rows)
         raw_tiles = []
         for g in range(GROUPS):
             for c in range(PASSES):
@@ -53,6 +53,8 @@ def tile_ternarylinear_s_kernel(tc, x, kernel, out):
                     out=raw[:], in_=kernel_passes[c, :, :, g * COLS : (g + 1) * COLS]
                 )
                 raw_tiles.append(raw)
+            if g == 0:
+                nc.sync.dma_start(out=x_sb[:], in_=x_rows)
 
         identity = keep.tile([P, P], F32)
         make_identity(nc, identity[:])
@@ -76,25 +78,25 @@ def tile_ternarylinear_s_kernel(tc, x, kernel, out):
 
         w_codes = keep.tile([P, CHUNKS, COLS], U32, align_bytes=64)
         w_scales = keep.tile([P, CHUNKS, COLS], U8, align_bytes=64)
-        sign_tiles = {}
+        rounded_tiles = {}
         grouped_tiles = {}
 
-        def sign_step(i):
-            above_low = sign_pool.tile([P, PACK, COLS], BF16, name="above_low")
-            nc.scalar.activation(
-                out=above_low[:], in_=raw_tiles[i][:], func=ACT.Sign, bias=THRESHOLD
-            )
-            sign_tiles[i] = above_low
-
-        def ternary_step(i):
-            grouped = grouped_pool.tile([P, COLS, PACK], BF16, name="grouped", align_bytes=64)
-            nc.vector.scalar_tensor_tensor(
-                out=grouped[:],
+        def round_step(i):
+            rounded = rounded_pool.tile([P, COLS, PACK], F32, name="rounded")
+            nc.vector.tensor_scalar(
+                out=rounded[:],
                 in0=raw_tiles[i][:].rearrange("p j n -> p n j"),
-                scalar=THRESHOLD,
-                in1=sign_tiles[i][:].rearrange("p j n -> p n j"),
-                op0=ALU.is_gt,
-                op1=ALU.min,
+                scalar1=INV_TWICE_THRESHOLD,
+                scalar2=ROUND_MAGIC,
+                op0=ALU.mult,
+                op1=ALU.add,
+            )
+            rounded_tiles[i] = rounded
+
+        def sign_step(i):
+            grouped = grouped_pool.tile([P, COLS, PACK], BF16, name="grouped", align_bytes=64)
+            nc.scalar.activation(
+                out=grouped[:], in_=rounded_tiles[i][:], func=ACT.Sign, bias=-ROUND_MAGIC
             )
             grouped_tiles[i] = grouped
 
@@ -118,7 +120,7 @@ def tile_ternarylinear_s_kernel(tc, x, kernel, out):
                     stop=(c == PASSES - 1),
                 )
             result = result_pool.tile([TOKENS, COLS], F32, name="result")
-            nc.scalar.copy(out=result[:], in_=acc[:])
+            nc.vector.tensor_copy(out=result[:], in_=acc[:])
             nc.sync.dma_start(out=out_rows[:, g * COLS : (g + 1) * COLS], in_=result[:])
 
         def finish_chunk(i):
@@ -126,12 +128,11 @@ def tile_ternarylinear_s_kernel(tc, x, kernel, out):
             if i % PASSES == PASSES - 1:
                 multiply_group(i // PASSES)
 
-        for i in range(SIGN_AHEAD):
-            sign_step(i)
+        round_step(0)
         for i in range(CHUNKS):
-            if i + SIGN_AHEAD < CHUNKS:
-                sign_step(i + SIGN_AHEAD)
-            ternary_step(i)
+            if i + 1 < CHUNKS:
+                round_step(i + 1)
+            sign_step(i)
             if i > 0:
                 finish_chunk(i - 1)
         finish_chunk(CHUNKS - 1)

@@ -1,3 +1,4 @@
+import math
 from contextlib import ExitStack
 
 from concourse import mybir
@@ -6,6 +7,7 @@ from concourse.masks import make_identity
 F32 = mybir.dt.float32
 BF16 = mybir.dt.bfloat16
 U32 = mybir.dt.uint32
+I32 = mybir.dt.int32
 U8 = mybir.dt.uint8
 FP8X4 = mybir.dt.float8_e4m3fn_x4
 ALU = mybir.AluOpType
@@ -23,8 +25,13 @@ THRESHOLD = 0.3
 COLS = 256
 GROUPS = N // COLS
 CHUNKS = GROUPS * PASSES
-INV_TWICE_THRESHOLD = 1.0 / (2.0 * THRESHOLD)
+LAST_ZERO = 153.0 / 512.0
+FIRST_ONE = 154.0 / 512.0
+MIDDLE = 0.5 + 2.0**-10
+TANH_SCALE = math.log((1.0 + MIDDLE) / (1.0 - MIDDLE)) / (LAST_ZERO + FIRST_ONE)
 ROUND_MAGIC = 1.5 * 2.0**23
+INV_TWICE_THRESHOLD = 1.0 / (2.0 * THRESHOLD)
+VECTOR_CHUNKS = (1, 5)
 
 FLOPS = 2 * TOKENS * K * N
 
@@ -39,6 +46,7 @@ def tile_ternarylinear_s_kernel(tc, x, kernel, out):
         keep = ctx.enter_context(tc.tile_pool(name="keep", bufs=1))
         raw_pool = ctx.enter_context(tc.tile_pool(name="raw", bufs=CHUNKS))
         rounded_pool = ctx.enter_context(tc.tile_pool(name="rounded", bufs=3))
+        integer_pool = ctx.enter_context(tc.tile_pool(name="integer", bufs=2))
         grouped_pool = ctx.enter_context(tc.tile_pool(name="grouped", bufs=3))
         result_pool = ctx.enter_context(tc.tile_pool(name="result", bufs=GROUPS))
         xt_pool = ctx.enter_context(tc.psum_pool(name="xt", bufs=1))
@@ -81,23 +89,38 @@ def tile_ternarylinear_s_kernel(tc, x, kernel, out):
         rounded_tiles = {}
         grouped_tiles = {}
 
-        def round_step(i):
-            rounded = rounded_pool.tile([P, COLS, PACK], F32, name="rounded")
-            nc.vector.tensor_scalar(
-                out=rounded[:],
-                in0=raw_tiles[i][:].rearrange("p j n -> p n j"),
-                scalar1=INV_TWICE_THRESHOLD,
-                scalar2=ROUND_MAGIC,
-                op0=ALU.mult,
-                op1=ALU.add,
-            )
+        def first_step(i):
+            by_word = raw_tiles[i][:].rearrange("p j n -> p n j")
+            if i in VECTOR_CHUNKS:
+                rounded = integer_pool.tile([P, COLS, PACK], I32, name="integer")
+                nc.vector.tensor_scalar(
+                    out=rounded[:],
+                    in0=by_word,
+                    scalar1=INV_TWICE_THRESHOLD,
+                    scalar2=1.0,
+                    op0=ALU.mult,
+                    op1=ALU.min,
+                )
+            else:
+                rounded = rounded_pool.tile([P, COLS, PACK], BF16, name="rounded")
+                nc.scalar.activation(
+                    out=rounded[:], in_=by_word, func=ACT.Tanh, scale=TANH_SCALE
+                )
             rounded_tiles[i] = rounded
 
-        def sign_step(i):
+        def second_step(i):
             grouped = grouped_pool.tile([P, COLS, PACK], BF16, name="grouped", align_bytes=64)
-            nc.scalar.activation(
-                out=grouped[:], in_=rounded_tiles[i][:], func=ACT.Sign, bias=-ROUND_MAGIC
-            )
+            if i in VECTOR_CHUNKS:
+                nc.vector.tensor_scalar_max(out=grouped[:], in0=rounded_tiles[i][:], scalar1=-1.0)
+            else:
+                nc.vector.tensor_scalar(
+                    out=grouped[:],
+                    in0=rounded_tiles[i][:],
+                    scalar1=ROUND_MAGIC,
+                    scalar2=ROUND_MAGIC,
+                    op0=ALU.add,
+                    op1=ALU.subtract,
+                )
             grouped_tiles[i] = grouped
 
         def quantise_step(i):
@@ -120,7 +143,7 @@ def tile_ternarylinear_s_kernel(tc, x, kernel, out):
                     stop=(c == PASSES - 1),
                 )
             result = result_pool.tile([TOKENS, COLS], F32, name="result")
-            nc.vector.tensor_copy(out=result[:], in_=acc[:])
+            nc.scalar.copy(out=result[:], in_=acc[:])
             nc.sync.dma_start(out=out_rows[:, g * COLS : (g + 1) * COLS], in_=result[:])
 
         def finish_chunk(i):
@@ -128,11 +151,11 @@ def tile_ternarylinear_s_kernel(tc, x, kernel, out):
             if i % PASSES == PASSES - 1:
                 multiply_group(i // PASSES)
 
-        round_step(0)
+        first_step(0)
         for i in range(CHUNKS):
             if i + 1 < CHUNKS:
-                round_step(i + 1)
-            sign_step(i)
+                first_step(i + 1)
+            second_step(i)
             if i > 0:
                 finish_chunk(i - 1)
         finish_chunk(CHUNKS - 1)

@@ -22,16 +22,16 @@ N = 1024
 PASSES = K // K_PASS
 THRESHOLD = 0.3
 
-COLS = 256
-GROUPS = N // COLS
-CHUNKS = GROUPS * PASSES
+LOADS = ((0, 256), (256, 256), (512, 512))
+PIECES = ((0, 256), (256, 256), (512, 256), (768, 128), (896, 128))
+VECTOR_PIECES = ((1, 0), (1, 3))
+
 LAST_ZERO = 153.0 / 512.0
 FIRST_ONE = 154.0 / 512.0
 MIDDLE = 0.5 + 2.0**-10
 TANH_SCALE = math.log((1.0 + MIDDLE) / (1.0 - MIDDLE)) / (LAST_ZERO + FIRST_ONE)
 ROUND_MAGIC = 1.5 * 2.0**23
 INV_TWICE_THRESHOLD = 1.0 / (2.0 * THRESHOLD)
-VECTOR_CHUNKS = (1, 5)
 
 FLOPS = 2 * TOKENS * K * N
 
@@ -44,118 +44,162 @@ def tile_ternarylinear_s_kernel(tc, x, kernel, out):
 
     with ExitStack() as ctx:
         keep = ctx.enter_context(tc.tile_pool(name="keep", bufs=1))
-        raw_pool = ctx.enter_context(tc.tile_pool(name="raw", bufs=CHUNKS))
-        rounded_pool = ctx.enter_context(tc.tile_pool(name="rounded", bufs=3))
-        integer_pool = ctx.enter_context(tc.tile_pool(name="integer", bufs=2))
-        grouped_pool = ctx.enter_context(tc.tile_pool(name="grouped", bufs=3))
-        result_pool = ctx.enter_context(tc.tile_pool(name="result", bufs=GROUPS))
         xt_pool = ctx.enter_context(tc.psum_pool(name="xt", bufs=1))
-        acc_pool = ctx.enter_context(tc.psum_pool(name="acc", bufs=GROUPS))
+        acc_pool = ctx.enter_context(tc.psum_pool(name="acc", bufs=1))
 
         x_sb = keep.tile([TOKENS, K], BF16)
-        raw_tiles = []
-        for g in range(GROUPS):
-            for c in range(PASSES):
-                raw = raw_pool.tile([P, PACK, COLS], BF16, name="raw")
-                nc.sync.dma_start(
-                    out=raw[:], in_=kernel_passes[c, :, :, g * COLS : (g + 1) * COLS]
-                )
-                raw_tiles.append(raw)
-            if g == 0:
+        raw_tiles = {}
+        for l, (n0, width) in enumerate(LOADS):
+            if l == 2:
                 nc.sync.dma_start(out=x_sb[:], in_=x_rows)
+            for c in range(PASSES):
+                raw = keep.tile([P, PACK, width], BF16, name=f"raw{c}_{l}")
+                nc.sync.dma_start(out=raw[:], in_=kernel_passes[c, :, :, n0 : n0 + width])
+                raw_tiles[c, l] = raw
 
         identity = keep.tile([P, P], F32)
         make_identity(nc, identity[:])
-        x_words = x_sb[:].bitcast(F32).rearrange("m (c p u) -> m c u p", c=PASSES, u=2)
-        xt = xt_pool.tile([P, PASSES, 2, TOKENS], F32)
-        for c in range(PASSES):
-            for u in range(2):
-                nc.tensor.transpose(xt[:, c, u, :], x_words[:, c, u, :], identity[:])
-        x_grouped = keep.tile([P, PASSES * TOKENS * PACK], BF16, align_bytes=64)
-        nc.vector.tensor_copy(
-            out=x_grouped[:].bitcast(F32).rearrange("p (c m u) -> p c m u", c=PASSES, u=2),
-            in_=xt[:].rearrange("p c u m -> p c m u"),
-        )
         x_codes = keep.tile([P, PASSES, TOKENS], U32, align_bytes=64)
         x_scales = keep.tile([P, PASSES, TOKENS], U8, align_bytes=64)
-        nc.vector.quantize_mx(
-            out=x_codes[:].rearrange("p c m -> p (c m)").bitcast(FP8X4),
-            scales=x_scales[:].rearrange("p c m -> p (c m)"),
-            in_=x_grouped[:],
-        )
 
-        w_codes = keep.tile([P, CHUNKS, COLS], U32, align_bytes=64)
-        w_scales = keep.tile([P, CHUNKS, COLS], U8, align_bytes=64)
+        def prepare_x():
+            x_words = x_sb[:].bitcast(F32).rearrange("m (c p u) -> m c u p", c=PASSES, u=2)
+            xt = xt_pool.tile([P, PASSES, 2, TOKENS], F32)
+            for c in range(PASSES):
+                for u in range(2):
+                    nc.tensor.transpose(xt[:, c, u, :], x_words[:, c, u, :], identity[:])
+            x_grouped = keep.tile([P, PASSES * TOKENS * PACK], BF16, align_bytes=64)
+            nc.scalar.copy(
+                out=x_grouped[:].bitcast(F32).rearrange("p (c m u) -> p c m u", c=PASSES, u=2),
+                in_=xt[:].rearrange("p c u m -> p c m u"),
+            )
+            return x_grouped
+
+        def quantise_x(x_grouped):
+            nc.vector.quantize_mx(
+                out=x_codes[:].rearrange("p c m -> p (c m)").bitcast(FP8X4),
+                scales=x_scales[:].rearrange("p c m -> p (c m)"),
+                in_=x_grouped[:],
+            )
+
         rounded_tiles = {}
         grouped_tiles = {}
+        w_codes = {}
+        w_scales = {}
 
-        def first_step(i):
-            by_word = raw_tiles[i][:].rearrange("p j n -> p n j")
-            if i in VECTOR_CHUNKS:
-                rounded = integer_pool.tile([P, COLS, PACK], I32, name="integer")
+        def raw_piece(c, r):
+            n0, width = PIECES[r]
+            for l, (load0, load_width) in enumerate(LOADS):
+                if load0 <= n0 < load0 + load_width:
+                    first = n0 - load0
+                    return raw_tiles[c, l][:, :, first : first + width].rearrange("p j n -> p n j")
+
+        def first_step(c, r):
+            width = PIECES[r][1]
+            if (c, r) in VECTOR_PIECES:
+                rounded = keep.tile([P, width, PACK], I32, name=f"integer{c}_{r}")
                 nc.vector.tensor_scalar(
                     out=rounded[:],
-                    in0=by_word,
+                    in0=raw_piece(c, r),
                     scalar1=INV_TWICE_THRESHOLD,
                     scalar2=1.0,
                     op0=ALU.mult,
                     op1=ALU.min,
                 )
             else:
-                rounded = rounded_pool.tile([P, COLS, PACK], BF16, name="rounded")
+                rounded = keep.tile([P, width, PACK], BF16, name=f"rounded{c}_{r}")
                 nc.scalar.activation(
-                    out=rounded[:], in_=by_word, func=ACT.Tanh, scale=TANH_SCALE
+                    out=rounded[:], in_=raw_piece(c, r), func=ACT.Tanh, scale=TANH_SCALE
                 )
-            rounded_tiles[i] = rounded
+            rounded_tiles[c, r] = rounded
 
-        def second_step(i):
-            grouped = grouped_pool.tile([P, COLS, PACK], BF16, name="grouped", align_bytes=64)
-            if i in VECTOR_CHUNKS:
-                nc.vector.tensor_scalar_max(out=grouped[:], in0=rounded_tiles[i][:], scalar1=-1.0)
+        def second_step(c, r):
+            width = PIECES[r][1]
+            grouped = keep.tile([P, width, PACK], BF16, name=f"grouped{c}_{r}", align_bytes=64)
+            if (c, r) in VECTOR_PIECES:
+                nc.vector.tensor_scalar_max(
+                    out=grouped[:], in0=rounded_tiles[c, r][:], scalar1=-1.0
+                )
             else:
                 nc.vector.tensor_scalar(
                     out=grouped[:],
-                    in0=rounded_tiles[i][:],
+                    in0=rounded_tiles[c, r][:],
                     scalar1=ROUND_MAGIC,
                     scalar2=ROUND_MAGIC,
                     op0=ALU.add,
                     op1=ALU.subtract,
                 )
-            grouped_tiles[i] = grouped
+            grouped_tiles[c, r] = grouped
 
-        def quantise_step(i):
+        def quantise_step(c, r):
+            width = PIECES[r][1]
+            codes = keep.tile([P, width], U32, name=f"codes{c}_{r}", align_bytes=64)
+            scales = keep.tile([P, width], U8, name=f"scales{c}_{r}", align_bytes=64)
             nc.vector.quantize_mx(
-                out=w_codes[:, i, :].bitcast(FP8X4),
-                scales=w_scales[:, i, :],
-                in_=grouped_tiles[i][:].rearrange("p n j -> p (n j)"),
+                out=codes[:].bitcast(FP8X4),
+                scales=scales[:],
+                in_=grouped_tiles[c, r][:].rearrange("p n j -> p (n j)"),
+            )
+            w_codes[c, r] = codes
+            w_scales[c, r] = scales
+
+        acc_tiles = {}
+
+        def multiply(c, r):
+            n0, width = PIECES[r]
+            if c == 0:
+                acc = acc_pool.tile([TOKENS, width], F32, name=f"acc{r}")
+                acc_tiles[r] = acc
+            nc.tensor.matmul_mx(
+                out=acc_tiles[r][:],
+                lhsT=x_codes[:, c, :].bitcast(FP8X4),
+                lhsT_scale=x_scales[:, c, :],
+                rhs=w_codes[c, r][:].bitcast(FP8X4),
+                rhs_scale=w_scales[c, r][:],
+                start=(c == 0),
+                stop=(c == PASSES - 1),
             )
 
-        def multiply_group(g):
-            acc = acc_pool.tile([TOKENS, COLS], F32, name="acc")
-            for c in range(PASSES):
-                nc.tensor.matmul_mx(
-                    out=acc[:],
-                    lhsT=x_codes[:, c, :].bitcast(FP8X4),
-                    lhsT_scale=x_scales[:, c, :],
-                    rhs=w_codes[:, g * PASSES + c, :].bitcast(FP8X4),
-                    rhs_scale=w_scales[:, g * PASSES + c, :],
-                    start=(c == 0),
-                    stop=(c == PASSES - 1),
-                )
-            result = result_pool.tile([TOKENS, COLS], F32, name="result")
-            nc.scalar.copy(out=result[:], in_=acc[:])
-            nc.sync.dma_start(out=out_rows[:, g * COLS : (g + 1) * COLS], in_=result[:])
+        def store(r):
+            n0, width = PIECES[r]
+            result = keep.tile([TOKENS, width], F32, name=f"result{r}")
+            nc.scalar.copy(out=result[:], in_=acc_tiles[r][:])
+            nc.sync.dma_start(out=out_rows[:, n0 : n0 + width], in_=result[:])
 
-        def finish_chunk(i):
-            quantise_step(i)
-            if i % PASSES == PASSES - 1:
-                multiply_group(i // PASSES)
-
-        first_step(0)
-        for i in range(CHUNKS):
-            if i + 1 < CHUNKS:
-                first_step(i + 1)
-            second_step(i)
-            if i > 0:
-                finish_chunk(i - 1)
-        finish_chunk(CHUNKS - 1)
+        with tc.manual_schedule():
+            first_step(0, 0)
+            first_step(1, 0)
+            first_step(0, 1)
+            second_step(0, 0)
+            second_step(1, 0)
+            first_step(1, 1)
+            quantise_step(0, 0)
+            quantise_step(1, 0)
+            second_step(0, 1)
+            quantise_step(0, 1)
+            x_grouped = prepare_x()
+            second_step(1, 1)
+            quantise_x(x_grouped)
+            quantise_step(1, 1)
+            first_step(0, 2)
+            first_step(1, 3)
+            first_step(1, 2)
+            second_step(0, 2)
+            second_step(1, 3)
+            quantise_step(0, 2)
+            quantise_step(1, 3)
+            first_step(0, 3)
+            second_step(1, 2)
+            quantise_step(1, 2)
+            first_step(0, 4)
+            second_step(0, 3)
+            quantise_step(0, 3)
+            first_step(1, 4)
+            second_step(0, 4)
+            quantise_step(0, 4)
+            second_step(1, 4)
+            quantise_step(1, 4)
+            for r in range(len(PIECES)):
+                multiply(0, r)
+                multiply(1, r)
+                store(r)

@@ -33,6 +33,8 @@ TANH_SCALE = math.log((1.0 + MIDDLE) / (1.0 - MIDDLE)) / (LAST_ZERO + FIRST_ONE)
 ROUND_MAGIC = 1.5 * 2.0**23
 INV_TWICE_THRESHOLD = 1.0 / (2.0 * THRESHOLD)
 
+RUN = 4
+
 FLOPS = 2 * TOKENS * K * N
 
 
@@ -92,7 +94,7 @@ def tile_ternarylinear_s_kernel(tc, x, kernel, out):
             for l, (load0, load_width) in enumerate(LOADS):
                 if load0 <= n0 < load0 + load_width:
                     first = n0 - load0
-                    return raw_tiles[c, l][:, :, first : first + width].rearrange("p j n -> p n j")
+                    return raw_tiles[c, l][:, :, first : first + width]
 
         def first_step(c, r):
             width = PIECES[r][1]
@@ -100,7 +102,7 @@ def tile_ternarylinear_s_kernel(tc, x, kernel, out):
                 rounded = keep.tile([P, width, PACK], I32, name=f"integer{c}_{r}")
                 nc.vector.tensor_scalar(
                     out=rounded[:],
-                    in0=raw_piece(c, r),
+                    in0=raw_piece(c, r).rearrange("p j n -> p n j"),
                     scalar1=INV_TWICE_THRESHOLD,
                     scalar2=1.0,
                     op0=ALU.mult,
@@ -109,7 +111,10 @@ def tile_ternarylinear_s_kernel(tc, x, kernel, out):
             else:
                 rounded = keep.tile([P, width, PACK], BF16, name=f"rounded{c}_{r}")
                 nc.scalar.activation(
-                    out=rounded[:], in_=raw_piece(c, r), func=ACT.Tanh, scale=TANH_SCALE
+                    out=rounded[:].rearrange("p (m i) j -> p m j i", i=RUN),
+                    in_=raw_piece(c, r).rearrange("p j (m i) -> p m j i", i=RUN),
+                    func=ACT.Tanh,
+                    scale=TANH_SCALE,
                 )
             rounded_tiles[c, r] = rounded
 

@@ -23,8 +23,7 @@ PASSES = K // K_PASS
 THRESHOLD = 0.3
 
 LOADS = ((0, 256), (256, 256), (512, 512))
-PIECES = ((0, 256), (256, 256), (512, 256), (768, 128), (896, 128))
-VECTOR_PIECES = ((1, 0), (1, 3))
+GROUPS = ((0, 256), (256, 256), (512, 256), (768, 128), (896, 128))
 
 LAST_ZERO = 153.0 / 512.0
 FIRST_ONE = 154.0 / 512.0
@@ -84,127 +83,137 @@ def tile_ternarylinear_s_kernel(tc, x, kernel, out):
                 in_=x_grouped[:],
             )
 
-        rounded_tiles = {}
-        grouped_tiles = {}
-        w_codes = {}
-        w_scales = {}
+        tanh_tiles = []
+        integer_tiles = []
+        grouped_tiles = []
+        w_codes = []
+        w_scales = []
+        for l, (n0, width) in enumerate(LOADS):
+            tanh_tile = keep.tile([P, PASSES, width, PACK], BF16, name=f"tanh{l}")
+            tanh_tiles.append(tanh_tile)
+            integer = keep.tile([P, PASSES, width, PACK], I32, name=f"integer{l}")
+            integer_tiles.append(integer)
+            grouped = keep.tile([P, PASSES, width, PACK], BF16, name=f"grouped{l}", align_bytes=64)
+            grouped_tiles.append(grouped)
+            codes = keep.tile([P, PASSES, width], U32, name=f"codes{l}", align_bytes=64)
+            w_codes.append(codes)
+            scales = keep.tile([P, PASSES, width], U8, name=f"scales{l}", align_bytes=64)
+            w_scales.append(scales)
 
-        def raw_piece(c, r):
-            n0, width = PIECES[r]
+        def tanh_step(c, l, cols):
+            nc.scalar.activation(
+                out=tanh_tiles[l][:, c, cols].rearrange("p (m i) j -> p m j i", i=RUN),
+                in_=raw_tiles[c, l][:, :, cols].rearrange("p j (m i) -> p m j i", i=RUN),
+                func=ACT.Tanh,
+                scale=TANH_SCALE,
+            )
+
+        def round_step(passes, l, cols):
+            nc.vector.tensor_scalar(
+                out=grouped_tiles[l][:, passes, cols],
+                in0=tanh_tiles[l][:, passes, cols],
+                scalar1=ROUND_MAGIC,
+                scalar2=ROUND_MAGIC,
+                op0=ALU.add,
+                op1=ALU.subtract,
+            )
+
+        def integer_step(c, l, cols):
+            nc.vector.tensor_scalar(
+                out=integer_tiles[l][:, c, cols],
+                in0=raw_tiles[c, l][:, :, cols].rearrange("p j n -> p n j"),
+                scalar1=INV_TWICE_THRESHOLD,
+                scalar2=1.0,
+                op0=ALU.mult,
+                op1=ALU.min,
+            )
+
+        def clip_step(passes, l, cols):
+            nc.vector.tensor_scalar_max(
+                out=grouped_tiles[l][:, passes, cols],
+                in0=integer_tiles[l][:, passes, cols],
+                scalar1=-1.0,
+            )
+
+        def quantise_step(passes, l, cols):
+            nc.vector.quantize_mx(
+                out=w_codes[l][:, passes, cols].rearrange("p c n -> p (c n)").bitcast(FP8X4),
+                scales=w_scales[l][:, passes, cols].rearrange("p c n -> p (c n)"),
+                in_=grouped_tiles[l][:, passes, cols].rearrange("p c n j -> p (c n j)"),
+            )
+
+        acc_tiles = []
+        for g, (n0, width) in enumerate(GROUPS):
+            acc = acc_pool.tile([TOKENS, width], F32, name=f"acc{g}")
+            acc_tiles.append(acc)
+
+        def multiply(c, g):
+            n0, width = GROUPS[g]
             for l, (load0, load_width) in enumerate(LOADS):
                 if load0 <= n0 < load0 + load_width:
-                    first = n0 - load0
-                    return raw_tiles[c, l][:, :, first : first + width]
+                    cols = slice(n0 - load0, n0 - load0 + width)
+                    nc.tensor.matmul_mx(
+                        out=acc_tiles[g][:],
+                        lhsT=x_codes[:, c, :].bitcast(FP8X4),
+                        lhsT_scale=x_scales[:, c, :],
+                        rhs=w_codes[l][:, c, cols].bitcast(FP8X4),
+                        rhs_scale=w_scales[l][:, c, cols],
+                        start=(c == 0),
+                        stop=(c == PASSES - 1),
+                    )
 
-        def first_step(c, r):
-            width = PIECES[r][1]
-            if (c, r) in VECTOR_PIECES:
-                rounded = keep.tile([P, width, PACK], I32, name=f"integer{c}_{r}")
-                nc.vector.tensor_scalar(
-                    out=rounded[:],
-                    in0=raw_piece(c, r).rearrange("p j n -> p n j"),
-                    scalar1=INV_TWICE_THRESHOLD,
-                    scalar2=1.0,
-                    op0=ALU.mult,
-                    op1=ALU.min,
-                )
-            else:
-                rounded = keep.tile([P, width, PACK], BF16, name=f"rounded{c}_{r}")
-                nc.scalar.activation(
-                    out=rounded[:].rearrange("p (m i) j -> p m j i", i=RUN),
-                    in_=raw_piece(c, r).rearrange("p j (m i) -> p m j i", i=RUN),
-                    func=ACT.Tanh,
-                    scale=TANH_SCALE,
-                )
-            rounded_tiles[c, r] = rounded
-
-        def second_step(c, r):
-            width = PIECES[r][1]
-            grouped = keep.tile([P, width, PACK], BF16, name=f"grouped{c}_{r}", align_bytes=64)
-            if (c, r) in VECTOR_PIECES:
-                nc.vector.tensor_scalar_max(
-                    out=grouped[:], in0=rounded_tiles[c, r][:], scalar1=-1.0
-                )
-            else:
-                nc.vector.tensor_scalar(
-                    out=grouped[:],
-                    in0=rounded_tiles[c, r][:],
-                    scalar1=ROUND_MAGIC,
-                    scalar2=ROUND_MAGIC,
-                    op0=ALU.add,
-                    op1=ALU.subtract,
-                )
-            grouped_tiles[c, r] = grouped
-
-        def quantise_step(c, r):
-            width = PIECES[r][1]
-            codes = keep.tile([P, width], U32, name=f"codes{c}_{r}", align_bytes=64)
-            scales = keep.tile([P, width], U8, name=f"scales{c}_{r}", align_bytes=64)
-            nc.vector.quantize_mx(
-                out=codes[:].bitcast(FP8X4),
-                scales=scales[:],
-                in_=grouped_tiles[c, r][:].rearrange("p n j -> p (n j)"),
-            )
-            w_codes[c, r] = codes
-            w_scales[c, r] = scales
-
-        acc_tiles = {}
-
-        def multiply(c, r):
-            n0, width = PIECES[r]
-            if c == 0:
-                acc = acc_pool.tile([TOKENS, width], F32, name=f"acc{r}")
-                acc_tiles[r] = acc
-            nc.tensor.matmul_mx(
-                out=acc_tiles[r][:],
-                lhsT=x_codes[:, c, :].bitcast(FP8X4),
-                lhsT_scale=x_scales[:, c, :],
-                rhs=w_codes[c, r][:].bitcast(FP8X4),
-                rhs_scale=w_scales[c, r][:],
-                start=(c == 0),
-                stop=(c == PASSES - 1),
-            )
-
-        def store(r):
-            n0, width = PIECES[r]
-            result = keep.tile([TOKENS, width], F32, name=f"result{r}")
-            nc.scalar.copy(out=result[:], in_=acc_tiles[r][:])
+        def store(g, copy):
+            n0, width = GROUPS[g]
+            result = keep.tile([TOKENS, width], F32, name=f"result{g}")
+            copy(out=result[:], in_=acc_tiles[g][:])
             nc.sync.dma_start(out=out_rows[:, n0 : n0 + width], in_=result[:])
 
+        BOTH = slice(0, PASSES)
+        FIRST = slice(0, 1)
+        SECOND = slice(1, 2)
         with tc.manual_schedule():
-            first_step(0, 0)
-            first_step(1, 0)
-            first_step(0, 1)
-            second_step(0, 0)
-            second_step(1, 0)
-            first_step(1, 1)
-            quantise_step(0, 0)
-            quantise_step(1, 0)
-            second_step(0, 1)
-            quantise_step(0, 1)
+            tanh_step(0, 0, slice(192, 256))
+            integer_step(0, 0, slice(0, 192))
+            tanh_step(1, 0, slice(192, 256))
+            integer_step(1, 0, slice(0, 192))
+            tanh_step(0, 1, slice(0, 256))
+            clip_step(BOTH, 0, slice(0, 192))
+            tanh_step(1, 1, slice(0, 256))
+            round_step(BOTH, 0, slice(192, 256))
             x_grouped = prepare_x()
-            second_step(1, 1)
+            quantise_step(BOTH, 0, slice(0, 256))
+            tanh_step(0, 2, slice(0, 256))
+            round_step(FIRST, 1, slice(0, 256))
+            tanh_step(0, 2, slice(256, 512))
+            quantise_step(FIRST, 1, slice(0, 256))
+            tanh_step(1, 2, slice(128, 384))
+            round_step(SECOND, 1, slice(0, 256))
+            tanh_step(1, 2, slice(384, 512))
             quantise_x(x_grouped)
-            quantise_step(1, 1)
-            first_step(0, 2)
-            first_step(1, 3)
-            first_step(1, 2)
-            second_step(0, 2)
-            second_step(1, 3)
-            quantise_step(0, 2)
-            quantise_step(1, 3)
-            first_step(0, 3)
-            second_step(1, 2)
-            quantise_step(1, 2)
-            first_step(0, 4)
-            second_step(0, 3)
-            quantise_step(0, 3)
-            first_step(1, 4)
-            second_step(0, 4)
-            quantise_step(0, 4)
-            second_step(1, 4)
-            quantise_step(1, 4)
-            for r in range(len(PIECES)):
-                multiply(0, r)
-                multiply(1, r)
-                store(r)
+            multiply(0, 0)
+            multiply(1, 0)
+            multiply(0, 1)
+            store(0, nc.scalar.copy)
+            quantise_step(SECOND, 1, slice(0, 256))
+            multiply(1, 1)
+            store(1, nc.scalar.copy)
+            integer_step(1, 2, slice(0, 128))
+            round_step(FIRST, 2, slice(0, 256))
+            clip_step(SECOND, 2, slice(0, 128))
+            quantise_step(FIRST, 2, slice(0, 256))
+            multiply(0, 2)
+            quantise_step(SECOND, 2, slice(0, 128))
+            round_step(FIRST, 2, slice(256, 512))
+            quantise_step(FIRST, 2, slice(256, 512))
+            multiply(0, 3)
+            multiply(0, 4)
+            round_step(SECOND, 2, slice(128, 384))
+            quantise_step(SECOND, 2, slice(128, 384))
+            multiply(1, 2)
+            multiply(1, 3)
+            store(2, nc.scalar.copy)
+            round_step(SECOND, 2, slice(384, 512))
+            store(3, nc.scalar.copy)
+            quantise_step(SECOND, 2, slice(384, 512))
+            multiply(1, 4)
+            store(4, nc.vector.tensor_copy)

@@ -172,23 +172,24 @@ def tile_ternarylinear_s_kernel(tc, x, kernel, out):
         FIRST = slice(0, 1)
         SECOND = slice(1, 2)
         with tc.manual_schedule():
-            tanh_step(0, 0, slice(192, 256))
-            integer_step(0, 0, slice(0, 192))
-            tanh_step(1, 0, slice(192, 256))
-            integer_step(1, 0, slice(0, 192))
+            tanh_step(0, 0, slice(160, 256))
+            integer_step(0, 0, slice(0, 160))
+            tanh_step(1, 0, slice(160, 256))
+            integer_step(1, 0, slice(0, 160))
             tanh_step(0, 1, slice(0, 256))
-            clip_step(BOTH, 0, slice(0, 192))
+            clip_step(BOTH, 0, slice(0, 160))
             tanh_step(1, 1, slice(0, 256))
-            round_step(BOTH, 0, slice(192, 256))
+            round_step(BOTH, 0, slice(160, 256))
             x_grouped = prepare_x()
             quantise_step(BOTH, 0, slice(0, 256))
             tanh_step(0, 2, slice(0, 256))
             round_step(FIRST, 1, slice(0, 256))
-            tanh_step(0, 2, slice(256, 512))
+            tanh_step(0, 2, slice(384, 512))
             quantise_step(FIRST, 1, slice(0, 256))
-            tanh_step(1, 2, slice(128, 384))
-            round_step(SECOND, 1, slice(0, 256))
+            tanh_step(1, 2, slice(0, 256))
+            integer_step(0, 2, slice(256, 384))
             tanh_step(1, 2, slice(384, 512))
+            round_step(SECOND, 1, slice(0, 256))
             quantise_x(x_grouped)
             multiply(0, 0)
             multiply(1, 0)
@@ -197,23 +198,23 @@ def tile_ternarylinear_s_kernel(tc, x, kernel, out):
             quantise_step(SECOND, 1, slice(0, 256))
             multiply(1, 1)
             store(1, nc.scalar.copy)
-            integer_step(1, 2, slice(0, 128))
+            integer_step(1, 2, slice(256, 384))
             round_step(FIRST, 2, slice(0, 256))
-            clip_step(SECOND, 2, slice(0, 128))
+            clip_step(BOTH, 2, slice(256, 384))
             quantise_step(FIRST, 2, slice(0, 256))
             multiply(0, 2)
-            quantise_step(SECOND, 2, slice(0, 128))
-            round_step(FIRST, 2, slice(256, 512))
+            quantise_step(SECOND, 2, slice(256, 384))
+            round_step(FIRST, 2, slice(384, 512))
             quantise_step(FIRST, 2, slice(256, 512))
             multiply(0, 3)
-            multiply(0, 4)
-            round_step(SECOND, 2, slice(128, 384))
-            quantise_step(SECOND, 2, slice(128, 384))
-            multiply(1, 2)
             multiply(1, 3)
+            multiply(0, 4)
+            store(3, nc.scalar.copy)
+            round_step(SECOND, 2, slice(0, 256))
+            quantise_step(SECOND, 2, slice(0, 256))
+            multiply(1, 2)
             store(2, nc.scalar.copy)
             round_step(SECOND, 2, slice(384, 512))
-            store(3, nc.scalar.copy)
             quantise_step(SECOND, 2, slice(384, 512))
             multiply(1, 4)
             store(4, nc.vector.tensor_copy)

@@ -187,9 +187,9 @@ def tile_ternarylinear_s_kernel(tc, x, kernel, out):
             tanh_step(0, 2, slice(384, 512))
             quantise_step(FIRST, 1, slice(0, 256))
             tanh_step(1, 2, slice(0, 256))
-            integer_step(0, 2, slice(256, 384))
-            tanh_step(1, 2, slice(384, 512))
             round_step(SECOND, 1, slice(0, 256))
+            tanh_step(1, 2, slice(384, 512))
+            integer_step(0, 2, slice(256, 384))
             quantise_x(x_grouped)
             multiply(0, 0)
             multiply(1, 0)
@@ -203,18 +203,18 @@ def tile_ternarylinear_s_kernel(tc, x, kernel, out):
             clip_step(BOTH, 2, slice(256, 384))
             quantise_step(FIRST, 2, slice(0, 256))
             multiply(0, 2)
-            quantise_step(SECOND, 2, slice(256, 384))
             round_step(FIRST, 2, slice(384, 512))
+            quantise_step(SECOND, 2, slice(256, 384))
             quantise_step(FIRST, 2, slice(256, 512))
             multiply(0, 3)
             multiply(1, 3)
             multiply(0, 4)
             store(3, nc.scalar.copy)
             round_step(SECOND, 2, slice(0, 256))
+            round_step(SECOND, 2, slice(384, 512))
             quantise_step(SECOND, 2, slice(0, 256))
             multiply(1, 2)
             store(2, nc.scalar.copy)
-            round_step(SECOND, 2, slice(384, 512))
             quantise_step(SECOND, 2, slice(384, 512))
             multiply(1, 4)
             store(4, nc.vector.tensor_copy)

@@ -177,16 +177,16 @@ def tile_ternarylinear_s_kernel(tc, x, kernel, out):
             tanh_step(1, 0, slice(160, 256))
             integer_step(1, 0, slice(0, 160))
             tanh_step(0, 1, slice(0, 256))
-            clip_step(BOTH, 0, slice(0, 160))
-            tanh_step(1, 1, slice(0, 256))
             round_step(BOTH, 0, slice(160, 256))
+            tanh_step(1, 1, slice(0, 256))
+            clip_step(BOTH, 0, slice(0, 160))
             x_grouped = prepare_x()
-            quantise_step(BOTH, 0, slice(0, 256))
-            tanh_step(0, 2, slice(0, 256))
             round_step(FIRST, 1, slice(0, 256))
-            tanh_step(0, 2, slice(384, 512))
-            quantise_step(FIRST, 1, slice(0, 256))
+            tanh_step(0, 2, slice(0, 256))
+            quantise_step(BOTH, 0, slice(0, 256))
             tanh_step(1, 2, slice(0, 256))
+            quantise_step(FIRST, 1, slice(0, 256))
+            tanh_step(0, 2, slice(384, 512))
             round_step(SECOND, 1, slice(0, 256))
             tanh_step(1, 2, slice(384, 512))
             integer_step(0, 2, slice(256, 384))
@@ -203,18 +203,19 @@ def tile_ternarylinear_s_kernel(tc, x, kernel, out):
             clip_step(BOTH, 2, slice(256, 384))
             quantise_step(FIRST, 2, slice(0, 256))
             multiply(0, 2)
-            round_step(FIRST, 2, slice(384, 512))
-            quantise_step(SECOND, 2, slice(256, 384))
-            quantise_step(FIRST, 2, slice(256, 512))
+            quantise_step(FIRST, 2, slice(256, 384))
             multiply(0, 3)
-            multiply(1, 3)
-            multiply(0, 4)
-            store(3, nc.scalar.copy)
             round_step(SECOND, 2, slice(0, 256))
-            round_step(SECOND, 2, slice(384, 512))
+            quantise_step(SECOND, 2, slice(256, 384))
+            multiply(1, 3)
+            store(3, nc.scalar.copy)
+            round_step(FIRST, 2, slice(384, 512))
             quantise_step(SECOND, 2, slice(0, 256))
             multiply(1, 2)
             store(2, nc.scalar.copy)
+            round_step(SECOND, 2, slice(384, 512))
+            quantise_step(FIRST, 2, slice(384, 512))
+            multiply(0, 4)
             quantise_step(SECOND, 2, slice(384, 512))
             multiply(1, 4)
             store(4, nc.vector.tensor_copy)

import math
from contextlib import ExitStack

from concourse import mybir
from concourse.masks import make_identity

F32 = mybir.dt.float32
BF16 = mybir.dt.bfloat16
U32 = mybir.dt.uint32
I32 = mybir.dt.int32
U8 = mybir.dt.uint8
FP8X4 = mybir.dt.float8_e4m3fn_x4
ALU = mybir.AluOpType
ACT = mybir.ActivationFunctionType

P = 128
PACK = 4
K_PASS = P * PACK
TOKENS = 128
K = 1024
N = 1024
PASSES = K // K_PASS
THRESHOLD = 0.3

LOADS = ((0, 256), (256, 256), (512, 512))
GROUPS = ((0, 256), (256, 256), (512, 256), (768, 128), (896, 128))

LAST_ZERO = 153.0 / 512.0
FIRST_ONE = 154.0 / 512.0
MIDDLE = 0.5 + 2.0**-10
TANH_SCALE = math.log((1.0 + MIDDLE) / (1.0 - MIDDLE)) / (LAST_ZERO + FIRST_ONE)
ROUND_MAGIC = 1.5 * 2.0**23
INV_TWICE_THRESHOLD = 1.0 / (2.0 * THRESHOLD)

RUN = 4

FLOPS = 2 * TOKENS * K * N


def tile_ternarylinear_s_kernel(tc, x, kernel, out):
    nc = tc.nc
    x_rows = x.flatten_outer_dims()
    out_rows = out.flatten_outer_dims()
    kernel_passes = kernel.rearrange("(c p j) n -> c p j n", p=P, j=PACK)

    with ExitStack() as ctx:
        keep = ctx.enter_context(tc.tile_pool(name="keep", bufs=1))
        xt_pool = ctx.enter_context(tc.psum_pool(name="xt", bufs=1))
        acc_pool = ctx.enter_context(tc.psum_pool(name="acc", bufs=1))

        x_sb = keep.tile([TOKENS, K], BF16)
        raw_tiles = {}
        for l, (n0, width) in enumerate(LOADS):
            if l == 2:
                nc.sync.dma_start(out=x_sb[:], in_=x_rows)
            for c in range(PASSES):
                raw = keep.tile([P, PACK, width], BF16, name=f"raw{c}_{l}")
                nc.sync.dma_start(out=raw[:], in_=kernel_passes[c, :, :, n0 : n0 + width])
                raw_tiles[c, l] = raw

        identity = keep.tile([P, P], F32)
        make_identity(nc, identity[:])
        x_codes = keep.tile([P, PASSES, TOKENS], U32, align_bytes=64)
        x_scales = keep.tile([P, PASSES, TOKENS], U8, align_bytes=64)

        def prepare_x():
            x_words = x_sb[:].bitcast(F32).rearrange("m (c p u) -> m c u p", c=PASSES, u=2)
            xt = xt_pool.tile([P, PASSES, 2, TOKENS], F32)
            for c in range(PASSES):
                for u in range(2):
                    nc.tensor.transpose(xt[:, c, u, :], x_words[:, c, u, :], identity[:])
            x_grouped = keep.tile([P, PASSES * TOKENS * PACK], BF16, align_bytes=64)
            nc.scalar.copy(
                out=x_grouped[:].bitcast(F32).rearrange("p (c m u) -> p c m u", c=PASSES, u=2),
                in_=xt[:].rearrange("p c u m -> p c m u"),
            )
            return x_grouped

        def quantise_x(x_grouped):
            nc.vector.quantize_mx(
                out=x_codes[:].rearrange("p c m -> p (c m)").bitcast(FP8X4),
                scales=x_scales[:].rearrange("p c m -> p (c m)"),
                in_=x_grouped[:],
            )

        tanh_tiles = []
        integer_tiles = []
        grouped_tiles = []
        w_codes = []
        w_scales = []
        for l, (n0, width) in enumerate(LOADS):
            tanh_tile = keep.tile([P, PASSES, width, PACK], BF16, name=f"tanh{l}")
            tanh_tiles.append(tanh_tile)
            integer = keep.tile([P, PASSES, width, PACK], I32, name=f"integer{l}")
            integer_tiles.append(integer)
            grouped = keep.tile([P, PASSES, width, PACK], BF16, name=f"grouped{l}", align_bytes=64)
            grouped_tiles.append(grouped)
            codes = keep.tile([P, PASSES, width], U32, name=f"codes{l}", align_bytes=64)
            w_codes.append(codes)
            scales = keep.tile([P, PASSES, width], U8, name=f"scales{l}", align_bytes=64)
            w_scales.append(scales)

        def tanh_step(c, l, cols):
            nc.scalar.activation(
                out=tanh_tiles[l][:, c, cols].rearrange("p (m i) j -> p m j i", i=RUN),
                in_=raw_tiles[c, l][:, :, cols].rearrange("p j (m i) -> p m j i", i=RUN),
                func=ACT.Tanh,
                scale=TANH_SCALE,
            )

        def round_step(passes, l, cols):
            nc.vector.tensor_scalar(
                out=grouped_tiles[l][:, passes, cols],
                in0=tanh_tiles[l][:, passes, cols],
                scalar1=ROUND_MAGIC,
                scalar2=ROUND_MAGIC,
                op0=ALU.add,
                op1=ALU.subtract,
            )

        def integer_step(c, l, cols):
            nc.vector.tensor_scalar(
                out=integer_tiles[l][:, c, cols],
                in0=raw_tiles[c, l][:, :, cols].rearrange("p j n -> p n j"),
                scalar1=INV_TWICE_THRESHOLD,
                scalar2=1.0,
                op0=ALU.mult,
                op1=ALU.min,
            )

        def clip_step(passes, l, cols):
            nc.vector.tensor_scalar_max(
                out=grouped_tiles[l][:, passes, cols],
                in0=integer_tiles[l][:, passes, cols],
                scalar1=-1.0,
            )

        def quantise_step(passes, l, cols):
            nc.vector.quantize_mx(
                out=w_codes[l][:, passes, cols].rearrange("p c n -> p (c n)").bitcast(FP8X4),
                scales=w_scales[l][:, passes, cols].rearrange("p c n -> p (c n)"),
                in_=grouped_tiles[l][:, passes, cols].rearrange("p c n j -> p (c n j)"),
            )

        acc_tiles = []
        for g, (n0, width) in enumerate(GROUPS):
            acc = acc_pool.tile([TOKENS, width], F32, name=f"acc{g}")
            acc_tiles.append(acc)

        def multiply(c, g):
            n0, width = GROUPS[g]
            for l, (load0, load_width) in enumerate(LOADS):
                if load0 <= n0 < load0 + load_width:
                    cols = slice(n0 - load0, n0 - load0 + width)
                    nc.tensor.matmul_mx(
                        out=acc_tiles[g][:],
                        lhsT=x_codes[:, c, :].bitcast(FP8X4),
                        lhsT_scale=x_scales[:, c, :],
                        rhs=w_codes[l][:, c, cols].bitcast(FP8X4),
                        rhs_scale=w_scales[l][:, c, cols],
                        start=(c == 0),
                        stop=(c == PASSES - 1),
                    )

        def store(g, copy):
            n0, width = GROUPS[g]
            result = keep.tile([TOKENS, width], F32, name=f"result{g}")
            copy(out=result[:], in_=acc_tiles[g][:])
            nc.sync.dma_start(out=out_rows[:, n0 : n0 + width], in_=result[:])

        BOTH = slice(0, PASSES)
        FIRST = slice(0, 1)
        SECOND = slice(1, 2)
        with tc.manual_schedule():
            tanh_step(0, 0, slice(160, 256))
            integer_step(0, 0, slice(0, 160))
            tanh_step(1, 0, slice(160, 256))
            integer_step(1, 0, slice(0, 160))
            tanh_step(0, 1, slice(0, 256))
            round_step(BOTH, 0, slice(160, 256))
            tanh_step(1, 1, slice(0, 256))
            clip_step(BOTH, 0, slice(0, 160))
            x_grouped = prepare_x()
            round_step(FIRST, 1, slice(0, 256))
            tanh_step(0, 2, slice(0, 256))
            quantise_step(BOTH, 0, slice(0, 256))
            tanh_step(1, 2, slice(0, 256))
            quantise_step(FIRST, 1, slice(0, 256))
            tanh_step(0, 2, slice(384, 512))
            round_step(SECOND, 1, slice(0, 256))
            tanh_step(1, 2, slice(384, 512))
            integer_step(0, 2, slice(256, 384))
            quantise_x(x_grouped)
            multiply(0, 0)
            multiply(1, 0)
            multiply(0, 1)
            store(0, nc.scalar.copy)
            quantise_step(SECOND, 1, slice(0, 256))
            multiply(1, 1)
            store(1, nc.scalar.copy)
            integer_step(1, 2, slice(256, 384))
            round_step(FIRST, 2, slice(0, 256))
            clip_step(BOTH, 2, slice(256, 384))
            quantise_step(FIRST, 2, slice(0, 256))
            multiply(0, 2)
            quantise_step(FIRST, 2, slice(256, 384))
            multiply(0, 3)
            round_step(SECOND, 2, slice(0, 256))
            quantise_step(SECOND, 2, slice(256, 384))
            multiply(1, 3)
            store(3, nc.scalar.copy)
            round_step(FIRST, 2, slice(384, 512))
            quantise_step(SECOND, 2, slice(0, 256))
            multiply(1, 2)
            store(2, nc.scalar.copy)
            round_step(SECOND, 2, slice(384, 512))
            quantise_step(FIRST, 2, slice(384, 512))
            multiply(0, 4)
            quantise_step(SECOND, 2, slice(384, 512))
            multiply(1, 4)
            store(4, nc.vector.tensor_copy)
